import numpy as np
import ml_dtypes

BF16 = ml_dtypes.bfloat16


def bf(x):
    return np.asarray(x, np.float32).astype(BF16)


def f32(x):
    return np.asarray(x, np.float32)


def f64(x):
    return np.asarray(x).astype(np.float64)


def striped(idx):
    return np.tile(idx.reshape(-1, 16).T, (8, 1))


C, S, N, A, R, K = 256, 256, 128, 8, 16, 128


def setup_inputs():
    base = f32(np.random.standard_normal((C, S)))
    q_lin = f32(np.random.standard_normal((C, N)))
    x = bf(np.random.standard_normal((C, N)))
    a_w = bf(np.random.standard_normal((C, K)) / np.sqrt(C))
    b_w = bf(np.random.standard_normal((K, C)) / np.sqrt(R))
    scal = f32(np.repeat(0.5 + np.random.random(A), R)[:, None])
    bins = np.random.permutation(np.tile(np.arange(A), N // A))
    mask = f32(np.repeat(bins[None, :] == np.arange(A)[:, None], R, axis=0))
    return {"base": base, "q_lin": q_lin, "x": x, "a_w": a_w, "b_w": b_w, "scal": scal, "mask": mask, "offs": striped(np.random.permutation(S)[:N])}


def reference(base, q_lin, x, a_w, b_w, scal, mask, offs):
    idx = offs[:16].T.reshape(-1)
    delta = (f64(a_w).T @ f64(x)) * f64(mask) * f64(scal)
    out = f64(base).copy()
    out[:, idx] = f64(q_lin) + f64(b_w).T @ delta
    return out

@@ -1,0 +1,63 @@
+import concourse.mybir as mybir
+
+P = 128
+C = 256
+S = 256
+N = 128
+K = 128
+BLOCKS = C // P
+
+FLOPS = 2 * C * K * N + 2 * K * C * N
+
+BF16, F32, U16 = mybir.dt.bfloat16, mybir.dt.float32, mybir.dt.uint16
+MULT, ADD = mybir.AluOpType.mult, mybir.AluOpType.add
+
+
+def tile_qkvparallellinearwithlora_s_kernel(tc, base, q_lin, x, a_w, b_w, scal, mask, offs, out):
+    nc = tc.nc
+    with (
+        tc.tile_pool(name="held", bufs=1) as held,
+        tc.psum_pool(name="psum", bufs=1) as psum,
+    ):
+        a_sb = held.tile([P, BLOCKS * K], BF16, name="a_sb")
+        x_sb = held.tile([P, BLOCKS * N], BF16, name="x_sb")
+        nc.sync.dma_start(a_sb[:], a_w.rearrange("(p h) k -> p (h k)", h=BLOCKS))
+        nc.scalar.dma_start(x_sb[:], x.rearrange("(p h) n -> p (h n)", h=BLOCKS))
+
+        offsets = held.tile([P, N // 16], U16, name="offsets")
+        nc.sync.dma_start(offsets[:], offs)
+
+        scal_sb = held.tile([P, 1], F32, name="scal_sb")
+        mask_sb = held.tile([P, N], F32, name="mask_sb")
+        b_sb = held.tile([P, C], BF16, name="b_sb")
+        nc.scalar.dma_start(scal_sb[:], scal)
+        nc.sync.dma_start(mask_sb[:], mask)
+        nc.scalar.dma_start(b_sb[:], b_w)
+
+        windows = [held.tile([P, S], F32, name=f"window{i}") for i in range(BLOCKS)]
+        q_sb = [held.tile([P, N], F32, name=f"q_sb{i}") for i in range(BLOCKS)]
+        for i in range(BLOCKS):
+            rows = slice(i * P, (i + 1) * P)
+            nc.sync.dma_start(windows[i][:], base[rows, :])
+            nc.scalar.dma_start(q_sb[i][:], q_lin[rows, :])
+
+        shrunk = psum.tile([K, N], F32, name="shrunk")
+        for h in range(BLOCKS):
+            nc.tensor.matmul(
+                shrunk[:],
+                a_sb[:, h * K : (h + 1) * K],
+                x_sb[:, h * N : (h + 1) * N],
+                start=(h == 0),
+                stop=(h == BLOCKS - 1),
+            )
+
+        delta = held.tile([K, N], BF16, name="delta")
+        nc.vector.scalar_tensor_tensor(delta[:], shrunk[:], scal_sb[:], mask_sb[:], MULT, MULT)
+
+        for i in range(BLOCKS):
+            upd_ps = psum.tile([P, N], F32, name=f"upd_ps{i}")
+            upd = held.tile([P, N], F32, name=f"upd{i}")
+            nc.tensor.matmul(upd_ps[:], b_sb[:, i * P : (i + 1) * P], delta[:], start=True, stop=True)
+            nc.vector.tensor_copy(upd[:], upd_ps[:])
+            nc.vector.tensor_tensor(windows[i][:].indirect(offsets[:]), q_sb[i][:], upd[:], ADD)
+            nc.sync.dma_start(out[i * P : (i + 1) * P, :], windows[i][:])

@@ -58,6 +58,9 @@ def tile_qkvparallellinearwithlora_s_kernel(tc, base, q_lin, x, a_w, b_w, scal, 
             upd_ps = psum.tile([P, N], F32, name=f"upd_ps{i}")
             upd = held.tile([P, N], F32, name=f"upd{i}")
             nc.tensor.matmul(upd_ps[:], b_sb[:, i * P : (i + 1) * P], delta[:], start=True, stop=True)
-            nc.vector.tensor_copy(upd[:], upd_ps[:])
+            if i == 0:
+                nc.vector.tensor_copy(upd[:], upd_ps[:])
+            else:
+                nc.scalar.copy(upd[:], upd_ps[:])
             nc.vector.tensor_tensor(windows[i][:].indirect(offsets[:]), q_sb[i][:], upd[:], ADD)
             nc.sync.dma_start(out[i * P : (i + 1) * P, :], windows[i][:])

@@ -24,9 +24,6 @@ def tile_qkvparallellinearwithlora_s_kernel(tc, base, q_lin, x, a_w, b_w, scal, 
         nc.sync.dma_start(a_sb[:], a_w.rearrange("(p h) k -> p (h k)", h=BLOCKS))
         nc.scalar.dma_start(x_sb[:], x.rearrange("(p h) n -> p (h n)", h=BLOCKS))
 
-        offsets = held.tile([P, N // 16], U16, name="offsets")
-        nc.sync.dma_start(offsets[:], offs)
-
         scal_sb = held.tile([P, 1], F32, name="scal_sb")
         mask_sb = held.tile([P, N], F32, name="mask_sb")
         b_sb = held.tile([P, C], BF16, name="b_sb")
@@ -34,12 +31,15 @@ def tile_qkvparallellinearwithlora_s_kernel(tc, base, q_lin, x, a_w, b_w, scal, 
         nc.sync.dma_start(mask_sb[:], mask)
         nc.scalar.dma_start(b_sb[:], b_w)
 
+        offsets = held.tile([P, N // 16], U16, name="offsets")
+        nc.sync.dma_start(offsets[:], offs)
+
         windows = [held.tile([P, S], F32, name=f"window{i}") for i in range(BLOCKS)]
         q_sb = [held.tile([P, N], F32, name=f"q_sb{i}") for i in range(BLOCKS)]
-        for i in range(BLOCKS):
-            rows = slice(i * P, (i + 1) * P)
-            nc.sync.dma_start(windows[i][:], base[rows, :])
-            nc.scalar.dma_start(q_sb[i][:], q_lin[rows, :])
+        nc.gpsimd.dma_start(q_sb[0][:], q_lin[0:P, :])
+        nc.sync.dma_start(windows[0][:], base[0:P, :])
+        nc.gpsimd.dma_start(q_sb[1][:], q_lin[P : 2 * P, :])
+        nc.gpsimd.dma_start(windows[1][:], base[P : 2 * P, :])
 
         shrunk = psum.tile([K, N], F32, name="shrunk")
         for h in range(BLOCKS):

@@ -21,25 +21,22 @@ def tile_qkvparallellinearwithlora_s_kernel(tc, base, q_lin, x, a_w, b_w, scal, 
     ):
         a_sb = held.tile([P, BLOCKS * K], BF16, name="a_sb")
         x_sb = held.tile([P, BLOCKS * N], BF16, name="x_sb")
-        nc.sync.dma_start(a_sb[:], a_w.rearrange("(p h) k -> p (h k)", h=BLOCKS))
-        nc.scalar.dma_start(x_sb[:], x.rearrange("(p h) n -> p (h n)", h=BLOCKS))
-
         scal_sb = held.tile([P, 1], F32, name="scal_sb")
         mask_sb = held.tile([P, N], F32, name="mask_sb")
         b_sb = held.tile([P, C], BF16, name="b_sb")
-        nc.scalar.dma_start(scal_sb[:], scal)
-        nc.sync.dma_start(mask_sb[:], mask)
-        nc.scalar.dma_start(b_sb[:], b_w)
-
         offsets = held.tile([P, N // 16], U16, name="offsets")
-        nc.sync.dma_start(offsets[:], offs)
-
         windows = [held.tile([P, S], F32, name=f"window{i}") for i in range(BLOCKS)]
-        q_sb = [held.tile([P, N], F32, name=f"q_sb{i}") for i in range(BLOCKS)]
-        nc.gpsimd.dma_start(q_sb[0][:], q_lin[0:P, :])
+        q_sb = held.tile([P, BLOCKS, N], F32, name="q_sb")
+
+        nc.sync.dma_start(a_sb[:], a_w.rearrange("(p h) k -> p (h k)", h=BLOCKS))
+        nc.scalar.dma_start(x_sb[:], x.rearrange("(p h) n -> p (h n)", h=BLOCKS))
+        nc.sync.dma_start(mask_sb[:], mask)
+        nc.scalar.dma_start(scal_sb[:], scal)
         nc.sync.dma_start(windows[0][:], base[0:P, :])
-        nc.gpsimd.dma_start(q_sb[1][:], q_lin[P : 2 * P, :])
-        nc.gpsimd.dma_start(windows[1][:], base[P : 2 * P, :])
+        nc.scalar.dma_start(b_sb[:], b_w)
+        nc.sync.dma_start(offsets[:], offs)
+        nc.scalar.dma_start(q_sb[:], q_lin.rearrange("(i p) n -> p i n", p=P))
+        nc.sync.dma_start(windows[1][:], base[P : 2 * P, :])
 
         shrunk = psum.tile([K, N], F32, name="shrunk")
         for h in range(BLOCKS):
@@ -54,13 +51,11 @@ def tile_qkvparallellinearwithlora_s_kernel(tc, base, q_lin, x, a_w, b_w, scal, 
         delta = held.tile([K, N], BF16, name="delta")
         nc.vector.scalar_tensor_tensor(delta[:], shrunk[:], scal_sb[:], mask_sb[:], MULT, MULT)
 
+        store_queues = [nc.sync, nc.scalar]
         for i in range(BLOCKS):
             upd_ps = psum.tile([P, N], F32, name=f"upd_ps{i}")
             upd = held.tile([P, N], F32, name=f"upd{i}")
             nc.tensor.matmul(upd_ps[:], b_sb[:, i * P : (i + 1) * P], delta[:], start=True, stop=True)
-            if i == 0:
-                nc.vector.tensor_copy(upd[:], upd_ps[:])
-            else:
-                nc.scalar.copy(upd[:], upd_ps[:])
-            nc.vector.tensor_tensor(windows[i][:].indirect(offsets[:]), q_sb[i][:], upd[:], ADD)
-            nc.sync.dma_start(out[i * P : (i + 1) * P, :], windows[i][:])
+            nc.vector.tensor_copy(upd[:], upd_ps[:])
+            nc.vector.tensor_tensor(windows[i][:].indirect(offsets[:]), q_sb[:, i, :], upd[:], ADD)
+            store_queues[i].dma_start(out[i * P : (i + 1) * P, :], windows[i][:])

@@ -51,7 +51,7 @@ def tile_qkvparallellinearwithlora_s_kernel(tc, base, q_lin, x, a_w, b_w, scal, 
         delta = held.tile([K, N], BF16, name="delta")
         nc.vector.scalar_tensor_tensor(delta[:], shrunk[:], scal_sb[:], mask_sb[:], MULT, MULT)
 
-        store_queues = [nc.sync, nc.scalar]
+        store_queues = [nc.scalar, nc.sync]
         for i in range(BLOCKS):
             upd_ps = psum.tile([P, N], F32, name=f"upd_ps{i}")
             upd = held.tile([P, N], F32, name=f"upd{i}")

@@ -56,6 +56,6 @@ def tile_qkvparallellinearwithlora_s_kernel(tc, base, q_lin, x, a_w, b_w, scal, 
             upd_ps = psum.tile([P, N], F32, name=f"upd_ps{i}")
             upd = held.tile([P, N], F32, name=f"upd{i}")
             nc.tensor.matmul(upd_ps[:], b_sb[:, i * P : (i + 1) * P], delta[:], start=True, stop=True)
-            nc.vector.tensor_copy(upd[:], upd_ps[:])
+            nc.scalar.copy(upd[:], upd_ps[:])
             nc.vector.tensor_tensor(windows[i][:].indirect(offsets[:]), q_sb[:, i, :], upd[:], ADD)
             store_queues[i].dma_start(out[i * P : (i + 1) * P, :], windows[i][:])

@@ -6,6 +6,8 @@ S = 256
 N = 128
 K = 128
 BLOCKS = C // P
+HALVES = 2
+NH = N // HALVES
 
 FLOPS = 2 * C * K * N + 2 * K * C * N
 
@@ -38,24 +40,30 @@ def tile_qkvparallellinearwithlora_s_kernel(tc, base, q_lin, x, a_w, b_w, scal, 
         nc.scalar.dma_start(q_sb[:], q_lin.rearrange("(i p) n -> p i n", p=P))
         nc.sync.dma_start(windows[1][:], base[P : 2 * P, :])
 
-        shrunk = psum.tile([K, N], F32, name="shrunk")
-        for h in range(BLOCKS):
-            nc.tensor.matmul(
-                shrunk[:],
-                a_sb[:, h * K : (h + 1) * K],
-                x_sb[:, h * N : (h + 1) * N],
-                start=(h == 0),
-                stop=(h == BLOCKS - 1),
-            )
 
-        delta = held.tile([K, N], BF16, name="delta")
-        nc.vector.scalar_tensor_tensor(delta[:], shrunk[:], scal_sb[:], mask_sb[:], MULT, MULT)
+        shrunk = [psum.tile([K, NH], F32, name=f"shrunk{t}") for t in range(HALVES)]
+        for h in range(BLOCKS):
+            for t in range(HALVES):
+                nc.tensor.matmul(
+                    shrunk[t][:],
+                    a_sb[:, h * K : (h + 1) * K],
+                    x_sb[:, h * N + t * NH : h * N + (t + 1) * NH],
+                    start=(h == 0),
+                    stop=(h == BLOCKS - 1),
+                )
+
+        delta = [held.tile([K, NH], BF16, name=f"delta{t}") for t in range(HALVES)]
+        for t in range(HALVES):
+            nc.vector.scalar_tensor_tensor(
+                delta[t][:], shrunk[t][:], scal_sb[:], mask_sb[:, t * NH : (t + 1) * NH], MULT, MULT
+            )
 
         store_queues = [nc.scalar, nc.sync]
         for i in range(BLOCKS):
-            upd_ps = psum.tile([P, N], F32, name=f"upd_ps{i}")
             upd = held.tile([P, N], F32, name=f"upd{i}")
-            nc.tensor.matmul(upd_ps[:], b_sb[:, i * P : (i + 1) * P], delta[:], start=True, stop=True)
-            nc.scalar.copy(upd[:], upd_ps[:])
+            for t in range(HALVES):
+                upd_ps = psum.tile([P, NH], F32, name=f"upd_ps{i}_{t}")
+                nc.tensor.matmul(upd_ps[:], b_sb[:, i * P : (i + 1) * P], delta[t][:], start=True, stop=True)
+                nc.scalar.copy(upd[:, t * NH : (t + 1) * NH], upd_ps[:])
             nc.vector.tensor_tensor(windows[i][:].indirect(offsets[:]), q_sb[:, i, :], upd[:], ADD)
             store_queues[i].dma_start(out[i * P : (i + 1) * P, :], windows[i][:])

@@ -6,8 +6,9 @@ S = 256
 N = 128
 K = 128
 BLOCKS = C // P
-HALVES = 2
-NH = N // HALVES
+PIECES = 4
+NP = N // PIECES
+PSUM_BANKS = 8
 
 FLOPS = 2 * C * K * N + 2 * K * C * N
 
@@ -19,7 +20,7 @@ def tile_qkvparallellinearwithlora_s_kernel(tc, base, q_lin, x, a_w, b_w, scal, 
     nc = tc.nc
     with (
         tc.tile_pool(name="held", bufs=1) as held,
-        tc.psum_pool(name="psum", bufs=1) as psum,
+        tc.psum_pool(name="psum", bufs=PSUM_BANKS) as psum,
     ):
         a_sb = held.tile([P, BLOCKS * K], BF16, name="a_sb")
         x_sb = held.tile([P, BLOCKS * N], BF16, name="x_sb")
@@ -41,29 +42,29 @@ def tile_qkvparallellinearwithlora_s_kernel(tc, base, q_lin, x, a_w, b_w, scal, 
         nc.sync.dma_start(windows[1][:], base[P : 2 * P, :])
 
 
-        shrunk = [psum.tile([K, NH], F32, name=f"shrunk{t}") for t in range(HALVES)]
-        for h in range(BLOCKS):
-            for t in range(HALVES):
+        shrunk = [psum.tile([K, NP], F32, name=f"shrunk{t}", tag="bank") for t in range(PIECES)]
+        for t in range(PIECES):
+            for h in range(BLOCKS):
                 nc.tensor.matmul(
                     shrunk[t][:],
                     a_sb[:, h * K : (h + 1) * K],
-                    x_sb[:, h * N + t * NH : h * N + (t + 1) * NH],
+                    x_sb[:, h * N + t * NP : h * N + (t + 1) * NP],
                     start=(h == 0),
                     stop=(h == BLOCKS - 1),
                 )
 
-        delta = [held.tile([K, NH], BF16, name=f"delta{t}") for t in range(HALVES)]
-        for t in range(HALVES):
+        delta = [held.tile([K, NP], BF16, name=f"delta{t}") for t in range(PIECES)]
+        for t in range(PIECES):
             nc.vector.scalar_tensor_tensor(
-                delta[t][:], shrunk[t][:], scal_sb[:], mask_sb[:, t * NH : (t + 1) * NH], MULT, MULT
+                delta[t][:], shrunk[t][:], scal_sb[:], mask_sb[:, t * NP : (t + 1) * NP], MULT, MULT
             )
 
         store_queues = [nc.scalar, nc.sync]
         for i in range(BLOCKS):
             upd = held.tile([P, N], F32, name=f"upd{i}")
-            for t in range(HALVES):
-                upd_ps = psum.tile([P, NH], F32, name=f"upd_ps{i}_{t}")
+            for t in range(PIECES):
+                upd_ps = psum.tile([P, NP], F32, name=f"upd_ps{i}_{t}", tag="bank")
                 nc.tensor.matmul(upd_ps[:], b_sb[:, i * P : (i + 1) * P], delta[t][:], start=True, stop=True)
-                nc.scalar.copy(upd[:, t * NH : (t + 1) * NH], upd_ps[:])
+                nc.scalar.copy(upd[:, t * NP : (t + 1) * NP], upd_ps[:])
             nc.vector.tensor_tensor(windows[i][:].indirect(offsets[:]), q_sb[:, i, :], upd[:], ADD)
             store_queues[i].dma_start(out[i * P : (i + 1) * P, :], windows[i][:])

@@ -29,17 +29,19 @@ def tile_qkvparallellinearwithlora_s_kernel(tc, base, q_lin, x, a_w, b_w, scal, 
         b_sb = held.tile([P, C], BF16, name="b_sb")
         offsets = held.tile([P, N // 16], U16, name="offsets")
         windows = [held.tile([P, S], F32, name=f"window{i}") for i in range(BLOCKS)]
-        q_sb = held.tile([P, BLOCKS, N], F32, name="q_sb")
+        q_sb = held.tile([P, BLOCKS * N], F32, name="q_sb")
+        base_blocks = base.rearrange("(p i) s -> i p s", i=BLOCKS)
+        out_blocks = out.rearrange("(p i) s -> i p s", i=BLOCKS)
 
         nc.sync.dma_start(a_sb[:], a_w.rearrange("(p h) k -> p (h k)", h=BLOCKS))
         nc.scalar.dma_start(x_sb[:], x.rearrange("(p h) n -> p (h n)", h=BLOCKS))
         nc.sync.dma_start(mask_sb[:], mask)
         nc.scalar.dma_start(scal_sb[:], scal)
-        nc.sync.dma_start(windows[0][:], base[0:P, :])
+        nc.sync.dma_start(windows[0][:], base_blocks[0])
         nc.scalar.dma_start(b_sb[:], b_w)
         nc.sync.dma_start(offsets[:], offs)
-        nc.scalar.dma_start(q_sb[:], q_lin.rearrange("(i p) n -> p i n", p=P))
-        nc.sync.dma_start(windows[1][:], base[P : 2 * P, :])
+        nc.scalar.dma_start(q_sb[:], q_lin.rearrange("(p i) n -> p (i n)", i=BLOCKS))
+        nc.sync.dma_start(windows[1][:], base_blocks[1])
 
 
         shrunk = [psum.tile([K, NP], F32, name=f"shrunk{t}", tag="bank") for t in range(PIECES)]
@@ -64,7 +66,7 @@ def tile_qkvparallellinearwithlora_s_kernel(tc, base, q_lin, x, a_w, b_w, scal, 
             upd = held.tile([P, N], F32, name=f"upd{i}")
             for t in range(PIECES):
                 upd_ps = psum.tile([P, NP], F32, name=f"upd_ps{i}_{t}", tag="bank")
-                nc.tensor.matmul(upd_ps[:], b_sb[:, i * P : (i + 1) * P], delta[t][:], start=True, stop=True)
+                nc.tensor.matmul(upd_ps[:], b_sb[:, i::BLOCKS], delta[t][:], start=True, stop=True)
                 nc.scalar.copy(upd[:, t * NP : (t + 1) * NP], upd_ps[:])
-            nc.vector.tensor_tensor(windows[i][:].indirect(offsets[:]), q_sb[:, i, :], upd[:], ADD)
-            store_queues[i].dma_start(out[i * P : (i + 1) * P, :], windows[i][:])
+            nc.vector.tensor_tensor(windows[i][:].indirect(offsets[:]), q_sb[:, i * N : (i + 1) * N], upd[:], ADD)
+            store_queues[i].dma_start(out_blocks[i], windows[i][:])

import concourse.mybir as mybir

P = 128
C = 256
S = 256
N = 128
K = 128
BLOCKS = C // P
PIECES = 4
NP = N // PIECES
PSUM_BANKS = 8

FLOPS = 2 * C * K * N + 2 * K * C * N

BF16, F32, U16 = mybir.dt.bfloat16, mybir.dt.float32, mybir.dt.uint16
MULT, ADD = mybir.AluOpType.mult, mybir.AluOpType.add


def tile_qkvparallellinearwithlora_s_kernel(tc, base, q_lin, x, a_w, b_w, scal, mask, offs, out):
    nc = tc.nc
    with (
        tc.tile_pool(name="held", bufs=1) as held,
        tc.psum_pool(name="psum", bufs=PSUM_BANKS) as psum,
    ):
        a_sb = held.tile([P, BLOCKS * K], BF16, name="a_sb")
        x_sb = held.tile([P, BLOCKS * N], BF16, name="x_sb")
        scal_sb = held.tile([P, 1], F32, name="scal_sb")
        mask_sb = held.tile([P, N], F32, name="mask_sb")
        b_sb = held.tile([P, C], BF16, name="b_sb")
        offsets = held.tile([P, N // 16], U16, name="offsets")
        windows = [held.tile([P, S], F32, name=f"window{i}") for i in range(BLOCKS)]
        q_sb = held.tile([P, BLOCKS * N], F32, name="q_sb")
        base_blocks = base.rearrange("(p i) s -> i p s", i=BLOCKS)
        out_blocks = out.rearrange("(p i) s -> i p s", i=BLOCKS)

        nc.sync.dma_start(a_sb[:], a_w.rearrange("(p h) k -> p (h k)", h=BLOCKS))
        nc.scalar.dma_start(x_sb[:], x.rearrange("(p h) n -> p (h n)", h=BLOCKS))
        nc.sync.dma_start(mask_sb[:], mask)
        nc.scalar.dma_start(scal_sb[:], scal)
        nc.sync.dma_start(windows[0][:], base_blocks[0])
        nc.scalar.dma_start(b_sb[:], b_w)
        nc.sync.dma_start(offsets[:], offs)
        nc.scalar.dma_start(q_sb[:], q_lin.rearrange("(p i) n -> p (i n)", i=BLOCKS))
        nc.sync.dma_start(windows[1][:], base_blocks[1])


        shrunk = [psum.tile([K, NP], F32, name=f"shrunk{t}", tag="bank") for t in range(PIECES)]
        for t in range(PIECES):
            for h in range(BLOCKS):
                nc.tensor.matmul(
                    shrunk[t][:],
                    a_sb[:, h * K : (h + 1) * K],
                    x_sb[:, h * N + t * NP : h * N + (t + 1) * NP],
                    start=(h == 0),
                    stop=(h == BLOCKS - 1),
                )

        delta = [held.tile([K, NP], BF16, name=f"delta{t}") for t in range(PIECES)]
        for t in range(PIECES):
            nc.vector.scalar_tensor_tensor(
                delta[t][:], shrunk[t][:], scal_sb[:], mask_sb[:, t * NP : (t + 1) * NP], MULT, MULT
            )

        store_queues = [nc.scalar, nc.sync]
        for i in range(BLOCKS):
            upd = held.tile([P, N], F32, name=f"upd{i}")
            for t in range(PIECES):
                upd_ps = psum.tile([P, NP], F32, name=f"upd_ps{i}_{t}", tag="bank")
                nc.tensor.matmul(upd_ps[:], b_sb[:, i::BLOCKS], delta[t][:], start=True, stop=True)
                nc.scalar.copy(upd[:, t * NP : (t + 1) * NP], upd_ps[:])
            nc.vector.tensor_tensor(windows[i][:].indirect(offsets[:]), q_sb[:, i * N : (i + 1) * N], upd[:], ADD)
            store_queues[i].dma_start(out_blocks[i], windows[i][:])
